import numpy as np
import ml_dtypes


def mxq(x, axis, fmt="e4m3"):
    dtype, down = {"e4m3": (ml_dtypes.float8_e4m3fn, 7), "e5m2": (ml_dtypes.float8_e5m2, 14)}[fmt]
    v = np.moveaxis(np.asarray(x, np.float32).astype(ml_dtypes.bfloat16).astype(np.float64), axis, -1)
    blocks = v.reshape(v.shape[:-1] + (-1, 32))
    amax = np.abs(blocks).max(-1, keepdims=True)
    byte = np.maximum(np.where(amax > 0, np.frexp(amax)[1] - 1 + 127, 0) - down, 1)
    scale = np.exp2(byte - 127.0)
    codes = (blocks / scale).astype(np.float32).astype(dtype).astype(np.float64)
    return np.moveaxis((codes * scale).reshape(v.shape), -1, axis)


WIDE = False


def mx_kscale(k):
    if not WIDE:
        return np.ones(k)
    levels = np.array([10, -10, 5, -5, 0])
    a = np.random.permutation(np.resize(levels, k // 512 * 4)).reshape(k // 512, 4)
    idx = np.arange(k)
    return np.exp2(a[idx // 512, idx % 128 // 32])


BF16 = ml_dtypes.bfloat16


def bf(x):
    return np.asarray(x, np.float32).astype(BF16)


def f64(x):
    return np.asarray(x).astype(np.float64)


E2M1 = np.array([0.0, 0.5, 1.0, 1.5, 2.0, 3.0, 4.0, 6.0, -0.0, -0.5, -1.0, -1.5, -2.0, -3.0, -4.0, -6.0])


def pack_weight(w, fmt):
    k, n = w.shape
    w = f64(bf(w)).reshape(k // 32, 32, n)
    amax = np.abs(w).max(1)
    if fmt == "e4m3":
        byte = np.frexp(amax)[1] - 1 + 127 - 7
    else:
        mant, ex = np.frexp(amax / 6.0)
        byte = np.where(mant > 0.5, ex, ex - 1) + 127
    byte = np.clip(np.where(amax > 0, byte, 1), 1, 254)
    scaled = (w * np.exp2(127.0 - byte)[:, None, :]).reshape(k, n).astype(np.float32)
    by_word = np.ascontiguousarray(scaled.reshape(k // 512, 128, 4, n).transpose(0, 1, 3, 2))
    if fmt == "e4m3":
        words = by_word.astype(ml_dtypes.float8_e4m3fn).view(np.uint8)
    else:
        c = by_word.astype(ml_dtypes.float4_e2m1fn).view(np.uint8) & 0xF
        words = c[..., 0::2] | (c[..., 1::2] << 4)
    return np.ascontiguousarray(words), np.ascontiguousarray(byte.astype(np.uint8).reshape(k // 512, 16, n))


def unpack_weight(words, scales, fmt):
    g, p, n, _ = words.shape
    if fmt == "e4m3":
        vals = np.ascontiguousarray(words).view(ml_dtypes.float8_e4m3fn).astype(np.float64)
    else:
        nib = np.empty((g, p, n, 4), np.uint8)
        nib[..., 0::2] = words & 0xF
        nib[..., 1::2] = words >> 4
        vals = E2M1[nib]
    vals = vals * np.repeat(np.exp2(scales.astype(np.float64) - 127.0), 8, axis=1)[..., None]
    return vals.transpose(0, 1, 3, 2).reshape(g * 512, n)

def pack4(w):
    words, scales = pack_weight(w, "e2m1")
    return words.reshape(words.shape[0], 128, -1), scales


def unpack4(words, scales):
    return unpack_weight(words.reshape(words.shape[0], 128, -1, 2), scales, "e2m1")


B, C, HH, WW, NH, HD, F = 2, 512, 16, 16, 8, 64, 512
EPS = 1e-5


def layer_norm(v, w, b):
    mu = v.mean(-1, keepdims=True)
    var = ((v - mu) ** 2).mean(-1, keepdims=True)
    return (v - mu) * (1.0 / np.sqrt(var + EPS)) * w + b


def setup_inputs():
    s = mx_kscale(F)
    h = bf(np.maximum(np.random.standard_normal((B, HH, WW, F)), 0.0) * 0.125 * s)
    ffn2_w = np.random.standard_normal((C, F)) * 0.5 / np.sqrt(F) / s
    words, scales = pack4(np.ascontiguousarray(ffn2_w.T))
    return {"h": h,
            "ffn2_w_words": words,
            "ffn2_w_scales": scales,
            "ffn2_b": bf(np.random.standard_normal(C) * 0.02),
            "scale_ffn": bf(0.1 * (1.0 + 0.1 * np.random.standard_normal(1))),
            "ln2_w": bf(1.0 + 0.1 * np.random.standard_normal(C)),
            "ln2_b": bf(0.1 * np.random.standard_normal(C)),
            "scale_norm2": bf(1.5 * (1.0 + 0.1 * np.random.standard_normal(1))),
            "x": bf(np.random.standard_normal((B, C, HH, WW)))}


def reference(h, ffn2_w_words, ffn2_w_scales, ffn2_b, scale_ffn, ln2_w, ln2_b, scale_norm2, x):
    y2 = ((mxq(f64(h), 3, "e4m3") @ unpack4(ffn2_w_words, ffn2_w_scales)) + f64(ffn2_b)) * f64(scale_ffn)
    y2 = layer_norm(y2, f64(ln2_w), f64(ln2_b)) * f64(scale_norm2)
    out = np.maximum(y2 + f64(x).transpose(0, 2, 3, 1), 0.0)
    return out.transpose(0, 3, 1, 2)

@@ -1,0 +1,177 @@
+from contextlib import ExitStack
+
+import concourse.mybir as mybir
+from concourse.masks import make_identity
+
+F32 = mybir.dt.float32
+BF16 = mybir.dt.bfloat16
+I32 = mybir.dt.int32
+U32 = mybir.dt.uint32
+U8 = mybir.dt.uint8
+FP8X4 = mybir.dt.float8_e4m3fn_x4
+FP4X4 = mybir.dt.float4_e2m1fn_x4
+ALU = mybir.AluOpType
+ACT = mybir.ActivationFunctionType
+
+P = 128
+K = 512
+C = 512
+PIXELS = 512
+IMAGE = 256
+N_TILES = PIXELS // P
+N_CB = C // P
+EPS = 1e-5
+
+FLOPS = 2 * PIXELS * K * C
+
+
+def tile_transformerconvblock_pc_s_kernel(
+    tc, h, ffn2_w_words, ffn2_w_scales, ffn2_b, scale_ffn, ln2_w, ln2_b, scale_norm2, x, out
+):
+    nc = tc.nc
+    h_rows = h.rearrange("b i j f -> (b i j) f")
+    x_view = x.rearrange("b (cb p) i j -> p (b cb) (i j)", p=P)
+    out_view = out.rearrange("b (cb p) i j -> p b cb (i j)", p=P)
+
+    with ExitStack() as ctx:
+        keep = ctx.enter_context(tc.tile_pool(name="keep", bufs=1))
+        work = ctx.enter_context(tc.tile_pool(name="work", bufs=N_TILES))
+        psum_once = ctx.enter_context(tc.psum_pool(name="psum_once", bufs=1))
+        psum = ctx.enter_context(tc.psum_pool(name="psum", bufs=2))
+
+        h_sb = keep.tile([P, N_TILES, K], BF16)
+        w_words = keep.tile([P, 2 * C], U8, align_bytes=64)
+        w_plane = keep.tile([P, C], U8, align_bytes=64)
+        x_sb = keep.tile([P, 2 * N_CB, IMAGE], BF16)
+
+        nc.vector.memset(w_plane[:].bitcast(I32), 0)
+
+        nc.sync.dma_start(out=h_sb[:, 0, :], in_=h_rows[0:P, :])
+        nc.sync.dma_start(out=w_words[:].bitcast(I32), in_=ffn2_w_words[0].bitcast(I32))
+        nc.sync.dma_start(out=h_sb[:, 1, :], in_=h_rows[P : 2 * P, :])
+        scale_rows = ffn2_w_scales[0].bitcast(I32)
+        for r in range(4):
+            nc.sync.dma_start(out=w_plane[r:P:32, :].bitcast(I32), in_=scale_rows[r:16:4, :])
+        nc.sync.dma_start(out=h_sb[:, 2, :], in_=h_rows[2 * P : 3 * P, :])
+        nc.sync.dma_start(out=h_sb[:, 3, :], in_=h_rows[3 * P : 4 * P, :])
+        nc.sync.dma_start(out=x_sb[:], in_=x_view)
+
+        bias_row = keep.tile([P, C], BF16)
+        nc.vector.memset(bias_row[:], 0.0)
+        nc.scalar.dma_start(out=bias_row[0:1, :], in_=ffn2_b.unsqueeze(0))
+        s_ffn = keep.tile([P, 1], BF16)
+        nc.scalar.dma_start(out=s_ffn[:], in_=scale_ffn.partition_broadcast(P))
+        s_norm = keep.tile([P, 1], BF16)
+        nc.scalar.dma_start(out=s_norm[:], in_=scale_norm2.partition_broadcast(P))
+
+        ident_f32 = keep.tile([P, P], F32)
+        make_identity(nc, ident_f32[:])
+        ln_rows = keep.tile([P, P], BF16)
+        nc.vector.memset(ln_rows[:], 0.0)
+        nc.gpsimd.dma_start(out=ln_rows[0:N_CB, :], in_=ln2_w.rearrange("(cb c) -> cb c", c=P))
+        nc.gpsimd.dma_start(out=ln_rows[N_CB : 2 * N_CB, :], in_=ln2_b.rearrange("(cb c) -> cb c", c=P))
+        ident_bf = keep.tile([P, P], BF16)
+        make_identity(nc, ident_bf[:])
+
+        one_col = keep.tile([P, 1], F32)
+        nc.vector.memset(one_col[:], 1.0)
+        warm = keep.tile([P, 1], F32)
+        nc.scalar.activation(out=warm[:], in_=one_col[:], func=ACT.Abs_reciprocal_sqrt)
+
+        ones = keep.tile([P, P], BF16)
+        nc.vector.memset(ones[:], 1.0)
+        bias_ps = psum_once.tile([P, C], F32)
+        nc.tensor.matmul(out=bias_ps[:], lhsT=ones[:], rhs=bias_row[:], start=True, stop=True)
+        bias_sb = keep.tile([P, C], F32)
+        nc.scalar.copy(out=bias_sb[:], in_=bias_ps[:])
+
+        k_col = keep.tile([P, 1], F32)
+        nc.vector.tensor_scalar(
+            out=k_col[:], in0=s_ffn[:], scalar1=s_ffn[:, 0:1], scalar2=1.0 / (C * EPS), op0=ALU.mult, op1=ALU.mult
+        )
+        gain = keep.tile([P, 1], F32)
+        nc.vector.tensor_scalar(
+            out=gain[:], in0=s_ffn[:], scalar1=s_norm[:, 0:1], scalar2=EPS**-0.5, op0=ALU.mult, op1=ALU.mult
+        )
+        ln_ps = psum_once.tile([P, P], BF16)
+        nc.tensor.transpose(ln_ps[:], ln_rows[:], ident_bf[:])
+        w_col = keep.tile([P, N_CB], F32)
+        nc.vector.tensor_scalar(
+            out=w_col[:], in0=ln_ps[:, 0:N_CB], scalar1=gain[:, 0:1], scalar2=None, op0=ALU.mult
+        )
+        b_col = keep.tile([P, N_CB], F32)
+        nc.vector.tensor_scalar(
+            out=b_col[:], in0=ln_ps[:, N_CB : 2 * N_CB], scalar1=s_norm[:, 0:1], scalar2=None, op0=ALU.mult
+        )
+
+        h_codes = keep.tile([P, N_TILES, P], U32, align_bytes=64)
+        h_scales = keep.tile([P, N_TILES, P], U8, align_bytes=64)
+
+        for i in range(N_TILES):
+            h_words = h_sb[:, i, :].bitcast(F32)
+            hT_ps = psum.tile([P, 2, P], F32)
+            for u in range(2):
+                nc.tensor.transpose(hT_ps[:, u, :], h_words[:, u : K // 2 : 2], ident_f32[:])
+            grouped = work.tile([P, 4 * P], BF16, align_bytes=64)
+            nc.scalar.copy(
+                out=grouped[:].bitcast(F32).rearrange("p (r u) -> p r u", u=2),
+                in_=hT_ps[:].rearrange("p u r -> p r u"),
+            )
+            nc.vector.quantize_mx(
+                out=h_codes[:, i, :].bitcast(FP8X4), scales=h_scales[:, i, :], in_=grouped[:]
+            )
+            acc = psum.tile([P, C], F32)
+            nc.tensor.matmul_mx(
+                out=acc[:],
+                lhsT=h_codes[:, i, :].bitcast(FP8X4),
+                lhsT_scale=h_scales[:, i, :],
+                rhs=w_words[:].bitcast(FP4X4),
+                rhs_scale=w_plane[:],
+                start=True,
+                stop=True,
+            )
+
+            v = work.tile([P, C], F32)
+            v_sum = work.tile([P, 1], F32)
+            nc.vector.scalar_tensor_tensor(
+                out=v[:], in0=acc[:], scalar=1.0, in1=bias_sb[:], op0=ALU.mult, op1=ALU.add, accum_out=v_sum[:]
+            )
+            neg_mean = work.tile([P, 1], F32)
+            nc.vector.tensor_scalar(
+                out=neg_mean[:], in0=v_sum[:], scalar1=-1.0 / C, scalar2=None, op0=ALU.mult
+            )
+            squares = work.tile([P, C], F32)
+            ssd = work.tile([P, 1], F32)
+            nc.scalar.activation(
+                out=squares[:], in_=v[:], func=ACT.Square, bias=neg_mean[:], scale=1.0, accum_out=ssd[:]
+            )
+            r_hat = work.tile([P, 1], F32)
+            nc.scalar.activation(
+                out=r_hat[:], in_=ssd[:], func=ACT.Abs_reciprocal_sqrt, bias=one_col[:], scale=k_col[:]
+            )
+            zn = work.tile([P, C], F32)
+            nc.gpsimd.tensor_scalar(
+                out=zn[:], in0=v[:], scalar1=neg_mean[:, 0:1], scalar2=r_hat[:, 0:1], op0=ALU.add, op1=ALU.mult
+            )
+
+            znT_ps = psum.tile([P, N_CB, P], F32)
+            for cb in range(N_CB):
+                nc.tensor.transpose(znT_ps[:, cb, :], zn[:, cb * P : (cb + 1) * P], ident_f32[:])
+            b = i // 2
+            cols = slice((i % 2) * P, (i % 2 + 1) * P)
+            summed = work.tile([P, N_CB, P], F32)
+            result = work.tile([P, N_CB, P], F32)
+            for cb in range(N_CB):
+                nc.vector.scalar_tensor_tensor(
+                    out=summed[:, cb, :],
+                    in0=znT_ps[:, cb, :],
+                    scalar=w_col[:, cb : cb + 1],
+                    in1=x_sb[:, b * N_CB + cb, cols],
+                    op0=ALU.mult,
+                    op1=ALU.add,
+                )
+            for cb in range(N_CB):
+                nc.scalar.activation(
+                    out=result[:, cb, :], in_=summed[:, cb, :], func=ACT.Relu, bias=b_col[:, cb : cb + 1], scale=1.0
+                )
+            nc.sync.dma_start(out=out_view[:, b, :, cols], in_=result[:])

@@ -36,80 +36,71 @@ def tile_transformerconvblock_pc_s_kernel(
     with ExitStack() as ctx:
         keep = ctx.enter_context(tc.tile_pool(name="keep", bufs=1))
         work = ctx.enter_context(tc.tile_pool(name="work", bufs=N_TILES))
-        psum_once = ctx.enter_context(tc.psum_pool(name="psum_once", bufs=1))
-        psum = ctx.enter_context(tc.psum_pool(name="psum", bufs=2))
+        psum = ctx.enter_context(tc.psum_pool(name="psum", bufs=8))
+        ctx.enter_context(tc.manual_schedule())
 
         h_sb = keep.tile([P, N_TILES, K], BF16)
         w_words = keep.tile([P, 2 * C], U8, align_bytes=64)
         w_plane = keep.tile([P, C], U8, align_bytes=64)
         x_sb = keep.tile([P, 2 * N_CB, IMAGE], BF16)
+        bias_row = keep.tile([P, C], BF16)
+        ln_rows = keep.tile([P, P], BF16)
+        s_ffn = keep.tile([P, 1], BF16)
+        s_norm = keep.tile([P, 1], BF16)
+        ones = keep.tile([P, P], BF16)
+        one_col = keep.tile([P, 1], F32)
 
+        nc.vector.memset(bias_row[:], 0.0)
         nc.vector.memset(w_plane[:].bitcast(I32), 0)
+        nc.vector.memset(one_col[:], 1.0)
+        nc.vector.memset(ones[:], 1.0)
+        nc.vector.memset(ln_rows[:], 0.0)
 
         nc.sync.dma_start(out=h_sb[:, 0, :], in_=h_rows[0:P, :])
-        nc.sync.dma_start(out=w_words[:].bitcast(I32), in_=ffn2_w_words[0].bitcast(I32))
-        nc.sync.dma_start(out=h_sb[:, 1, :], in_=h_rows[P : 2 * P, :])
+        nc.scalar.dma_start(out=bias_row[0:1, :], in_=ffn2_b.unsqueeze(0))
         scale_rows = ffn2_w_scales[0].bitcast(I32)
         for r in range(4):
             nc.sync.dma_start(out=w_plane[r:P:32, :].bitcast(I32), in_=scale_rows[r:16:4, :])
-        nc.sync.dma_start(out=h_sb[:, 2, :], in_=h_rows[2 * P : 3 * P, :])
-        nc.sync.dma_start(out=h_sb[:, 3, :], in_=h_rows[3 * P : 4 * P, :])
+        nc.sync.dma_start(
+            out=h_sb[:, 1:N_TILES, :], in_=h_rows[P:PIXELS, :].rearrange("(t p) k -> p t k", p=P)
+        )
+        nc.sync.dma_start(out=w_words[:].bitcast(I32), in_=ffn2_w_words[0].bitcast(I32))
+        nc.sync.dma_start(out=s_ffn[:], in_=scale_ffn.partition_broadcast(P))
+        nc.sync.dma_start(out=s_norm[:], in_=scale_norm2.partition_broadcast(P))
+        nc.sync.dma_start(out=ln_rows[0:N_CB, :], in_=ln2_w.rearrange("(cb c) -> cb c", c=P))
+        nc.sync.dma_start(out=ln_rows[N_CB : 2 * N_CB, :], in_=ln2_b.rearrange("(cb c) -> cb c", c=P))
         nc.sync.dma_start(out=x_sb[:], in_=x_view)
 
-        bias_row = keep.tile([P, C], BF16)
-        nc.vector.memset(bias_row[:], 0.0)
-        nc.scalar.dma_start(out=bias_row[0:1, :], in_=ffn2_b.unsqueeze(0))
-        s_ffn = keep.tile([P, 1], BF16)
-        nc.scalar.dma_start(out=s_ffn[:], in_=scale_ffn.partition_broadcast(P))
-        s_norm = keep.tile([P, 1], BF16)
-        nc.scalar.dma_start(out=s_norm[:], in_=scale_norm2.partition_broadcast(P))
-
         ident_f32 = keep.tile([P, P], F32)
-        make_identity(nc, ident_f32[:])
-        ln_rows = keep.tile([P, P], BF16)
-        nc.vector.memset(ln_rows[:], 0.0)
-        nc.gpsimd.dma_start(out=ln_rows[0:N_CB, :], in_=ln2_w.rearrange("(cb c) -> cb c", c=P))
-        nc.gpsimd.dma_start(out=ln_rows[N_CB : 2 * N_CB, :], in_=ln2_b.rearrange("(cb c) -> cb c", c=P))
         ident_bf = keep.tile([P, P], BF16)
+        make_identity(nc, ident_f32[:])
         make_identity(nc, ident_bf[:])
 
-        one_col = keep.tile([P, 1], F32)
-        nc.vector.memset(one_col[:], 1.0)
         warm = keep.tile([P, 1], F32)
         nc.scalar.activation(out=warm[:], in_=one_col[:], func=ACT.Abs_reciprocal_sqrt)
 
-        ones = keep.tile([P, P], BF16)
-        nc.vector.memset(ones[:], 1.0)
-        bias_ps = psum_once.tile([P, C], F32)
-        nc.tensor.matmul(out=bias_ps[:], lhsT=ones[:], rhs=bias_row[:], start=True, stop=True)
-        bias_sb = keep.tile([P, C], F32)
-        nc.scalar.copy(out=bias_sb[:], in_=bias_ps[:])
-
         k_col = keep.tile([P, 1], F32)
-        nc.vector.tensor_scalar(
-            out=k_col[:], in0=s_ffn[:], scalar1=s_ffn[:, 0:1], scalar2=1.0 / (C * EPS), op0=ALU.mult, op1=ALU.mult
+        nc.gpsimd.tensor_scalar(
+            out=k_col[:], in0=s_ffn[:], scalar1=s_ffn[:, 0:1], scalar2=1.0 / (C**3 * EPS), op0=ALU.mult, op1=ALU.mult
         )
         gain = keep.tile([P, 1], F32)
-        nc.vector.tensor_scalar(
+        nc.gpsimd.tensor_scalar(
             out=gain[:], in0=s_ffn[:], scalar1=s_norm[:, 0:1], scalar2=EPS**-0.5, op0=ALU.mult, op1=ALU.mult
-        )
-        ln_ps = psum_once.tile([P, P], BF16)
-        nc.tensor.transpose(ln_ps[:], ln_rows[:], ident_bf[:])
-        w_col = keep.tile([P, N_CB], F32)
-        nc.vector.tensor_scalar(
-            out=w_col[:], in0=ln_ps[:, 0:N_CB], scalar1=gain[:, 0:1], scalar2=None, op0=ALU.mult
-        )
-        b_col = keep.tile([P, N_CB], F32)
-        nc.vector.tensor_scalar(
-            out=b_col[:], in0=ln_ps[:, N_CB : 2 * N_CB], scalar1=s_norm[:, 0:1], scalar2=None, op0=ALU.mult
         )
 
         h_codes = keep.tile([P, N_TILES, P], U32, align_bytes=64)
         h_scales = keep.tile([P, N_TILES, P], U8, align_bytes=64)
+        bias_sb = keep.tile([P, C], F32)
+        w_col = keep.tile([P, N_CB], F32)
+        b_col = keep.tile([P, N_CB], F32)
+        v = [work.tile([P, C], F32, name="v") for i in range(N_TILES)]
+        v_sum = [work.tile([P, 1], F32, name="v_sum") for i in range(N_TILES)]
+        neg_mean = [work.tile([P, 1], F32, name="neg_mean") for i in range(N_TILES)]
+        r_hat = [work.tile([P, 1], F32, name="r_hat") for i in range(N_TILES)]
 
-        for i in range(N_TILES):
+        def turn_and_quantise(i):
             h_words = h_sb[:, i, :].bitcast(F32)
-            hT_ps = psum.tile([P, 2, P], F32)
+            hT_ps = psum.tile([P, 2, P], F32, tag="bank")
             for u in range(2):
                 nc.tensor.transpose(hT_ps[:, u, :], h_words[:, u : K // 2 : 2], ident_f32[:])
             grouped = work.tile([P, 4 * P], BF16, align_bytes=64)
@@ -120,7 +111,14 @@ def tile_transformerconvblock_pc_s_kernel(
             nc.vector.quantize_mx(
                 out=h_codes[:, i, :].bitcast(FP8X4), scales=h_scales[:, i, :], in_=grouped[:]
             )
-            acc = psum.tile([P, C], F32)
+
+        def spread_bias():
+            bias_ps = psum.tile([P, C], F32, tag="bank")
+            nc.tensor.matmul(out=bias_ps[:], lhsT=ones[:], rhs=bias_row[:], start=True, stop=True)
+            nc.scalar.copy(out=bias_sb[:], in_=bias_ps[:])
+
+        def multiply_and_sum(i):
+            acc = psum.tile([P, C], F32, tag="bank")
             nc.tensor.matmul_mx(
                 out=acc[:],
                 lhsT=h_codes[:, i, :].bitcast(FP8X4),
@@ -130,37 +128,42 @@ def tile_transformerconvblock_pc_s_kernel(
                 start=True,
                 stop=True,
             )
-
-            v = work.tile([P, C], F32)
-            v_sum = work.tile([P, 1], F32)
             nc.vector.scalar_tensor_tensor(
-                out=v[:], in0=acc[:], scalar=1.0, in1=bias_sb[:], op0=ALU.mult, op1=ALU.add, accum_out=v_sum[:]
+                out=v[i][:], in0=acc[:], scalar=1.0, in1=bias_sb[:], op0=ALU.mult, op1=ALU.add, accum_out=v_sum[i][:]
             )
-            neg_mean = work.tile([P, 1], F32)
+
+        def channel_columns():
+            ln_ps = psum.tile([P, P], BF16, tag="bank")
+            nc.tensor.transpose(ln_ps[:], ln_rows[:], ident_bf[:])
             nc.vector.tensor_scalar(
-                out=neg_mean[:], in0=v_sum[:], scalar1=-1.0 / C, scalar2=None, op0=ALU.mult
+                out=w_col[:], in0=ln_ps[:, 0:N_CB], scalar1=gain[:, 0:1], scalar2=None, op0=ALU.mult
             )
+            nc.vector.tensor_scalar(
+                out=b_col[:], in0=ln_ps[:, N_CB : 2 * N_CB], scalar1=s_norm[:, 0:1], scalar2=None, op0=ALU.mult
+            )
+
+        def sum_squares(i):
             squares = work.tile([P, C], F32)
             ssd = work.tile([P, 1], F32)
             nc.scalar.activation(
-                out=squares[:], in_=v[:], func=ACT.Square, bias=neg_mean[:], scale=1.0, accum_out=ssd[:]
+                out=squares[:], in_=v[i][:], func=ACT.Square, bias=v_sum[i][:], scale=-1.0 * C, accum_out=ssd[:]
             )
-            r_hat = work.tile([P, 1], F32)
+            nc.scalar.mul(out=neg_mean[i][:], in_=v_sum[i][:], mul=-1.0 / C)
             nc.scalar.activation(
-                out=r_hat[:], in_=ssd[:], func=ACT.Abs_reciprocal_sqrt, bias=one_col[:], scale=k_col[:]
-            )
-            zn = work.tile([P, C], F32)
-            nc.gpsimd.tensor_scalar(
-                out=zn[:], in0=v[:], scalar1=neg_mean[:, 0:1], scalar2=r_hat[:, 0:1], op0=ALU.add, op1=ALU.mult
+                out=r_hat[i][:], in_=ssd[:], func=ACT.Abs_reciprocal_sqrt, bias=one_col[:], scale=k_col[:]
             )
 
-            znT_ps = psum.tile([P, N_CB, P], F32)
+        def normalise_and_finish(i):
+            zn = work.tile([P, C], F32)
+            nc.gpsimd.tensor_scalar(
+                out=zn[:], in0=v[i][:], scalar1=neg_mean[i][:, 0:1], scalar2=r_hat[i][:, 0:1], op0=ALU.add, op1=ALU.mult
+            )
+            znT_ps = psum.tile([P, N_CB, P], F32, tag="bank")
             for cb in range(N_CB):
                 nc.tensor.transpose(znT_ps[:, cb, :], zn[:, cb * P : (cb + 1) * P], ident_f32[:])
             b = i // 2
             cols = slice((i % 2) * P, (i % 2 + 1) * P)
             summed = work.tile([P, N_CB, P], F32)
-            result = work.tile([P, N_CB, P], F32)
             for cb in range(N_CB):
                 nc.vector.scalar_tensor_tensor(
                     out=summed[:, cb, :],
@@ -170,8 +173,21 @@ def tile_transformerconvblock_pc_s_kernel(
                     op0=ALU.mult,
                     op1=ALU.add,
                 )
+            result = work.tile([P, N_CB, P], F32)
             for cb in range(N_CB):
                 nc.scalar.activation(
                     out=result[:, cb, :], in_=summed[:, cb, :], func=ACT.Relu, bias=b_col[:, cb : cb + 1], scale=1.0
                 )
             nc.sync.dma_start(out=out_view[:, b, :, cols], in_=result[:])
+
+        turn_and_quantise(0)
+        spread_bias()
+        for i in range(1, N_TILES):
+            turn_and_quantise(i)
+        for i in range(N_TILES):
+            multiply_and_sum(i)
+        channel_columns()
+        for i in range(N_TILES):
+            sum_squares(i)
+        for i in range(N_TILES):
+            normalise_and_finish(i)

@@ -22,6 +22,8 @@ N_TILES = PIXELS // P
 N_CB = C // P
 EPS = 1e-5
 
+FINISH_LAG = 1
+
 FLOPS = 2 * PIXELS * K * C
 
 
@@ -153,41 +155,53 @@ def tile_transformerconvblock_pc_s_kernel(
                 out=r_hat[i][:], in_=ssd[:], func=ACT.Abs_reciprocal_sqrt, bias=one_col[:], scale=k_col[:]
             )
 
-        def normalise_and_finish(i):
+        def normalise_and_turn(i):
             zn = work.tile([P, C], F32)
-            nc.gpsimd.tensor_scalar(
+            nc.vector.tensor_scalar(
                 out=zn[:], in0=v[i][:], scalar1=neg_mean[i][:, 0:1], scalar2=r_hat[i][:, 0:1], op0=ALU.add, op1=ALU.mult
             )
-            znT_ps = psum.tile([P, N_CB, P], F32, tag="bank")
+            blocks = []
             for cb in range(N_CB):
-                nc.tensor.transpose(znT_ps[:, cb, :], zn[:, cb * P : (cb + 1) * P], ident_f32[:])
+                znT_ps = psum.tile([P, P], F32, tag="bank")
+                nc.tensor.transpose(znT_ps[:], zn[:, cb * P : (cb + 1) * P], ident_f32[:])
+                blocks.append(znT_ps)
+            return blocks
+
+        def finish(i, blocks):
             b = i // 2
             cols = slice((i % 2) * P, (i % 2 + 1) * P)
             summed = work.tile([P, N_CB, P], F32)
+            result = work.tile([P, N_CB, P], F32)
             for cb in range(N_CB):
                 nc.vector.scalar_tensor_tensor(
                     out=summed[:, cb, :],
-                    in0=znT_ps[:, cb, :],
+                    in0=blocks[cb][:],
                     scalar=w_col[:, cb : cb + 1],
                     in1=x_sb[:, b * N_CB + cb, cols],
                     op0=ALU.mult,
                     op1=ALU.add,
                 )
-            result = work.tile([P, N_CB, P], F32)
-            for cb in range(N_CB):
-                nc.scalar.activation(
-                    out=result[:, cb, :], in_=summed[:, cb, :], func=ACT.Relu, bias=b_col[:, cb : cb + 1], scale=1.0
-                )
-            nc.sync.dma_start(out=out_view[:, b, :, cols], in_=result[:])
+            for first in range(0, N_CB, 2):
+                for cb in range(first, first + 2):
+                    nc.scalar.activation(
+                        out=result[:, cb, :], in_=summed[:, cb, :], func=ACT.Relu, bias=b_col[:, cb : cb + 1], scale=1.0
+                    )
+                nc.sync.dma_start(out=out_view[:, b, first : first + 2, cols], in_=result[:, first : first + 2, :])
 
         turn_and_quantise(0)
         spread_bias()
-        for i in range(1, N_TILES):
+        turn_and_quantise(1)
+        multiply_and_sum(0)
+        for i in range(2, N_TILES):
             turn_and_quantise(i)
-        for i in range(N_TILES):
+        for i in range(1, N_TILES):
             multiply_and_sum(i)
         channel_columns()
         for i in range(N_TILES):
             sum_squares(i)
-        for i in range(N_TILES):
-            normalise_and_finish(i)
+        turned = []
+        for i in range(N_TILES + FINISH_LAG):
+            if i < N_TILES:
+                turned.append(normalise_and_turn(i))
+            if i >= FINISH_LAG:
+                finish(i - FINISH_LAG, turned[i - FINISH_LAG])

@@ -20,9 +20,8 @@ PIXELS = 512
 IMAGE = 256
 N_TILES = PIXELS // P
 N_CB = C // P
+HALF = N_CB // 2
 EPS = 1e-5
-
-FINISH_LAG = 1
 
 FLOPS = 2 * PIXELS * K * C
 
@@ -60,13 +59,13 @@ def tile_transformerconvblock_pc_s_kernel(
 
         nc.sync.dma_start(out=h_sb[:, 0, :], in_=h_rows[0:P, :])
         nc.scalar.dma_start(out=bias_row[0:1, :], in_=ffn2_b.unsqueeze(0))
-        scale_rows = ffn2_w_scales[0].bitcast(I32)
-        for r in range(4):
-            nc.sync.dma_start(out=w_plane[r:P:32, :].bitcast(I32), in_=scale_rows[r:16:4, :])
         nc.sync.dma_start(
             out=h_sb[:, 1:N_TILES, :], in_=h_rows[P:PIXELS, :].rearrange("(t p) k -> p t k", p=P)
         )
         nc.sync.dma_start(out=w_words[:].bitcast(I32), in_=ffn2_w_words[0].bitcast(I32))
+        scale_rows = ffn2_w_scales[0].bitcast(I32)
+        for r in range(4):
+            nc.sync.dma_start(out=w_plane[r:P:32, :].bitcast(I32), in_=scale_rows[r:16:4, :])
         nc.sync.dma_start(out=s_ffn[:], in_=scale_ffn.partition_broadcast(P))
         nc.sync.dma_start(out=s_norm[:], in_=scale_norm2.partition_broadcast(P))
         nc.sync.dma_start(out=ln_rows[0:N_CB, :], in_=ln2_w.rearrange("(cb c) -> cb c", c=P))
@@ -157,7 +156,7 @@ def tile_transformerconvblock_pc_s_kernel(
 
         def normalise_and_turn(i):
             zn = work.tile([P, C], F32)
-            nc.vector.tensor_scalar(
+            nc.gpsimd.tensor_scalar(
                 out=zn[:], in0=v[i][:], scalar1=neg_mean[i][:, 0:1], scalar2=r_hat[i][:, 0:1], op0=ALU.add, op1=ALU.mult
             )
             blocks = []
@@ -181,27 +180,30 @@ def tile_transformerconvblock_pc_s_kernel(
                     op0=ALU.mult,
                     op1=ALU.add,
                 )
-            for first in range(0, N_CB, 2):
-                for cb in range(first, first + 2):
-                    nc.scalar.activation(
-                        out=result[:, cb, :], in_=summed[:, cb, :], func=ACT.Relu, bias=b_col[:, cb : cb + 1], scale=1.0
-                    )
-                nc.sync.dma_start(out=out_view[:, b, first : first + 2, cols], in_=result[:, first : first + 2, :])
+            for cb in range(HALF):
+                nc.scalar.activation(
+                    out=result[:, cb, :], in_=summed[:, cb, :], func=ACT.Relu, bias=b_col[:, cb : cb + 1], scale=1.0
+                )
+            nc.sync.dma_start(out=out_view[:, b, 0:HALF, cols], in_=result[:, 0:HALF, :])
+            for cb in range(HALF, N_CB):
+                nc.vector.tensor_scalar(
+                    out=result[:, cb, :],
+                    in0=summed[:, cb, :],
+                    scalar1=b_col[:, cb : cb + 1],
+                    scalar2=0.0,
+                    op0=ALU.add,
+                    op1=ALU.max,
+                )
+            nc.sync.dma_start(out=out_view[:, b, HALF:N_CB, cols], in_=result[:, HALF:N_CB, :])
 
         turn_and_quantise(0)
         spread_bias()
-        turn_and_quantise(1)
-        multiply_and_sum(0)
-        for i in range(2, N_TILES):
-            turn_and_quantise(i)
         for i in range(1, N_TILES):
+            turn_and_quantise(i)
+        for i in range(N_TILES):
             multiply_and_sum(i)
         channel_columns()
         for i in range(N_TILES):
             sum_squares(i)
-        turned = []
-        for i in range(N_TILES + FINISH_LAG):
-            if i < N_TILES:
-                turned.append(normalise_and_turn(i))
-            if i >= FINISH_LAG:
-                finish(i - FINISH_LAG, turned[i - FINISH_LAG])
+        for i in range(N_TILES):
+            finish(i, normalise_and_turn(i))

@@ -186,13 +186,8 @@ def tile_transformerconvblock_pc_s_kernel(
                 )
             nc.sync.dma_start(out=out_view[:, b, 0:HALF, cols], in_=result[:, 0:HALF, :])
             for cb in range(HALF, N_CB):
-                nc.vector.tensor_scalar(
-                    out=result[:, cb, :],
-                    in0=summed[:, cb, :],
-                    scalar1=b_col[:, cb : cb + 1],
-                    scalar2=0.0,
-                    op0=ALU.add,
-                    op1=ALU.max,
+                nc.scalar.activation(
+                    out=result[:, cb, :], in_=summed[:, cb, :], func=ACT.Relu, bias=b_col[:, cb : cb + 1], scale=1.0
                 )
             nc.sync.dma_start(out=out_view[:, b, HALF:N_CB, cols], in_=result[:, HALF:N_CB, :])
 

@@ -77,6 +77,10 @@ def tile_transformerconvblock_pc_s_kernel(
         make_identity(nc, ident_f32[:])
         make_identity(nc, ident_bf[:])
 
+        for w in range(2):
+            warm_ps = psum.tile([P, P], F32, tag="bank")
+            nc.tensor.matmul(out=warm_ps[:], lhsT=ident_f32[:], rhs=ident_f32[:], start=True, stop=True)
+
         warm = keep.tile([P, 1], F32)
         nc.scalar.activation(out=warm[:], in_=one_col[:], func=ACT.Abs_reciprocal_sqrt)
 

@@ -103,7 +103,7 @@ def tile_transformerconvblock_pc_s_kernel(
         neg_mean = [work.tile([P, 1], F32, name="neg_mean") for i in range(N_TILES)]
         r_hat = [work.tile([P, 1], F32, name="r_hat") for i in range(N_TILES)]
 
-        def turn_and_quantise(i):
+        def turn(i):
             h_words = h_sb[:, i, :].bitcast(F32)
             hT_ps = psum.tile([P, 2, P], F32, tag="bank")
             for u in range(2):
@@ -113,6 +113,9 @@ def tile_transformerconvblock_pc_s_kernel(
                 out=grouped[:].bitcast(F32).rearrange("p (r u) -> p r u", u=2),
                 in_=hT_ps[:].rearrange("p u r -> p r u"),
             )
+            return grouped
+
+        def quantise(i, grouped):
             nc.vector.quantize_mx(
                 out=h_codes[:, i, :].bitcast(FP8X4), scales=h_scales[:, i, :], in_=grouped[:]
             )
@@ -120,9 +123,9 @@ def tile_transformerconvblock_pc_s_kernel(
         def spread_bias():
             bias_ps = psum.tile([P, C], F32, tag="bank")
             nc.tensor.matmul(out=bias_ps[:], lhsT=ones[:], rhs=bias_row[:], start=True, stop=True)
-            nc.scalar.copy(out=bias_sb[:], in_=bias_ps[:])
+            return bias_ps
 
-        def multiply_and_sum(i):
+        def multiply(i):
             acc = psum.tile([P, C], F32, tag="bank")
             nc.tensor.matmul_mx(
                 out=acc[:],
@@ -133,6 +136,9 @@ def tile_transformerconvblock_pc_s_kernel(
                 start=True,
                 stop=True,
             )
+            return acc
+
+        def add_bias(i, acc):
             nc.vector.scalar_tensor_tensor(
                 out=v[i][:], in0=acc[:], scalar=1.0, in1=bias_sb[:], op0=ALU.mult, op1=ALU.add, accum_out=v_sum[i][:]
             )
@@ -195,12 +201,24 @@ def tile_transformerconvblock_pc_s_kernel(
                 )
             nc.sync.dma_start(out=out_view[:, b, HALF:N_CB, cols], in_=result[:, HALF:N_CB, :])
 
-        turn_and_quantise(0)
-        spread_bias()
-        for i in range(1, N_TILES):
-            turn_and_quantise(i)
-        for i in range(N_TILES):
-            multiply_and_sum(i)
+        g0 = turn(0)
+        bias_ps = spread_bias()
+        quantise(0, g0)
+        nc.vector.tensor_copy(out=bias_sb[:], in_=bias_ps[:])
+        g1 = turn(1)
+        g2 = turn(2)
+        g3 = turn(3)
+        quantise(1, g1)
+        quantise(2, g2)
+        acc0 = multiply(0)
+        add_bias(0, acc0)
+        quantise(3, g3)
+        acc1 = multiply(1)
+        add_bias(1, acc1)
+        acc2 = multiply(2)
+        add_bias(2, acc2)
+        acc3 = multiply(3)
+        add_bias(3, acc3)
         channel_columns()
         for i in range(N_TILES):
             sum_squares(i)

@@ -77,9 +77,11 @@ def tile_transformerconvblock_pc_s_kernel(
         make_identity(nc, ident_f32[:])
         make_identity(nc, ident_bf[:])
 
-        for w in range(2):
+        for width in (P, P, 44):
             warm_ps = psum.tile([P, P], F32, tag="bank")
-            nc.tensor.matmul(out=warm_ps[:], lhsT=ident_f32[:], rhs=ident_f32[:], start=True, stop=True)
+            nc.tensor.matmul(
+                out=warm_ps[:, 0:width], lhsT=ident_f32[:], rhs=ident_f32[:, 0:width], start=True, stop=True
+            )
 
         warm = keep.tile([P, 1], F32)
         nc.scalar.activation(out=warm[:], in_=one_col[:], func=ACT.Abs_reciprocal_sqrt)

@@ -95,6 +95,7 @@ def tile_transformerconvblock_pc_s_kernel(
             out=gain[:], in0=s_ffn[:], scalar1=s_norm[:, 0:1], scalar2=EPS**-0.5, op0=ALU.mult, op1=ALU.mult
         )
 
+        image = keep.tile([P, N_CB, IMAGE], F32)
         h_codes = keep.tile([P, N_TILES, P], U32, align_bytes=64)
         h_scales = keep.tile([P, N_TILES, P], U8, align_bytes=64)
         bias_sb = keep.tile([P, C], F32)
@@ -182,6 +183,27 @@ def tile_transformerconvblock_pc_s_kernel(
             b = i // 2
             cols = slice((i % 2) * P, (i % 2 + 1) * P)
             summed = work.tile([P, N_CB, P], F32)
+            if b == 1:
+                for cb in range(N_CB):
+                    nc.vector.scalar_tensor_tensor(
+                        out=summed[:, cb, :],
+                        in0=blocks[cb][:],
+                        scalar=w_col[:, cb : cb + 1],
+                        in1=x_sb[:, b * N_CB + cb, cols],
+                        op0=ALU.mult,
+                        op1=ALU.add,
+                    )
+                for cb in range(N_CB):
+                    nc.scalar.activation(
+                        out=image[:, cb, cols],
+                        in_=summed[:, cb, :],
+                        func=ACT.Relu,
+                        bias=b_col[:, cb : cb + 1],
+                        scale=1.0,
+                    )
+                    if i == N_TILES - 1:
+                        nc.sync.dma_start(out=out_view[:, b, cb, :], in_=image[:, cb, :])
+                return
             result = work.tile([P, N_CB, P], F32)
             for cb in range(N_CB):
                 nc.vector.scalar_tensor_tensor(

@@ -50,8 +50,10 @@ def tile_transformerconvblock_pc_s_kernel(
         s_norm = keep.tile([P, 1], BF16)
         ones = keep.tile([P, P], BF16)
         one_col = keep.tile([P, 1], F32)
+        warm_sb = keep.tile([P, P], F32)
 
-        nc.vector.memset(bias_row[:], 0.0)
+        nc.vector.memset(warm_sb[:], 1.0)
+        nc.vector.memset(bias_row[:].bitcast(F32), 0.0)
         nc.vector.memset(w_plane[:].bitcast(I32), 0)
         nc.vector.memset(one_col[:], 1.0)
         nc.vector.memset(ones[:], 1.0)
@@ -80,7 +82,7 @@ def tile_transformerconvblock_pc_s_kernel(
         for width in (P, P, 44):
             warm_ps = psum.tile([P, P], F32, tag="bank")
             nc.tensor.matmul(
-                out=warm_ps[:, 0:width], lhsT=ident_f32[:], rhs=ident_f32[:, 0:width], start=True, stop=True
+                out=warm_ps[:, 0:width], lhsT=warm_sb[:], rhs=warm_sb[:, 0:width], start=True, stop=True
             )
 
         warm = keep.tile([P, 1], F32)
@@ -95,13 +97,15 @@ def tile_transformerconvblock_pc_s_kernel(
             out=gain[:], in0=s_ffn[:], scalar1=s_norm[:, 0:1], scalar2=EPS**-0.5, op0=ALU.mult, op1=ALU.mult
         )
 
-        image = keep.tile([P, N_CB, IMAGE], F32)
+        result = keep.tile([P, 2, N_CB, IMAGE], F32)
         h_codes = keep.tile([P, N_TILES, P], U32, align_bytes=64)
         h_scales = keep.tile([P, N_TILES, P], U8, align_bytes=64)
-        bias_sb = keep.tile([P, C], F32)
+        bias_sb = keep.tile([P, C], BF16)
         w_col = keep.tile([P, N_CB], F32)
         b_col = keep.tile([P, N_CB], F32)
         v = [work.tile([P, C], F32, name="v") for i in range(N_TILES)]
+        zn = [work.tile([P, C], F32, name="zn") for i in range(N_TILES)]
+        summed = [work.tile([P, N_CB, P], F32, name="summed") for i in range(N_TILES)]
         v_sum = [work.tile([P, 1], F32, name="v_sum") for i in range(N_TILES)]
         neg_mean = [work.tile([P, 1], F32, name="neg_mean") for i in range(N_TILES)]
         r_hat = [work.tile([P, 1], F32, name="r_hat") for i in range(N_TILES)]
@@ -124,7 +128,7 @@ def tile_transformerconvblock_pc_s_kernel(
             )
 
         def spread_bias():
-            bias_ps = psum.tile([P, C], F32, tag="bank")
+            bias_ps = psum.tile([P, C], BF16, tag="bank")
             nc.tensor.matmul(out=bias_ps[:], lhsT=ones[:], rhs=bias_row[:], start=True, stop=True)
             return bias_ps
 
@@ -163,88 +167,108 @@ def tile_transformerconvblock_pc_s_kernel(
                 out=squares[:], in_=v[i][:], func=ACT.Square, bias=v_sum[i][:], scale=-1.0 * C, accum_out=ssd[:]
             )
             nc.scalar.mul(out=neg_mean[i][:], in_=v_sum[i][:], mul=-1.0 / C)
+            return ssd
+
+        def inverse_deviation(i, ssd):
             nc.scalar.activation(
                 out=r_hat[i][:], in_=ssd[:], func=ACT.Abs_reciprocal_sqrt, bias=one_col[:], scale=k_col[:]
             )
 
-        def normalise_and_turn(i):
-            zn = work.tile([P, C], F32)
-            nc.gpsimd.tensor_scalar(
-                out=zn[:], in0=v[i][:], scalar1=neg_mean[i][:, 0:1], scalar2=r_hat[i][:, 0:1], op0=ALU.add, op1=ALU.mult
+        def normalise(i, engine, cols=slice(0, C)):
+            engine.tensor_scalar(
+                out=zn[i][:, cols],
+                in0=v[i][:, cols],
+                scalar1=neg_mean[i][:, 0:1],
+                scalar2=r_hat[i][:, 0:1],
+                op0=ALU.add,
+                op1=ALU.mult,
             )
+
+        def turn_back(i):
             blocks = []
             for cb in range(N_CB):
                 znT_ps = psum.tile([P, P], F32, tag="bank")
-                nc.tensor.transpose(znT_ps[:], zn[:, cb * P : (cb + 1) * P], ident_f32[:])
+                nc.tensor.transpose(znT_ps[:], zn[i][:, cb * P : (cb + 1) * P], ident_f32[:])
                 blocks.append(znT_ps)
             return blocks
 
-        def finish(i, blocks):
-            b = i // 2
-            cols = slice((i % 2) * P, (i % 2 + 1) * P)
-            summed = work.tile([P, N_CB, P], F32)
-            if b == 1:
-                for cb in range(N_CB):
-                    nc.vector.scalar_tensor_tensor(
-                        out=summed[:, cb, :],
-                        in0=blocks[cb][:],
-                        scalar=w_col[:, cb : cb + 1],
-                        in1=x_sb[:, b * N_CB + cb, cols],
-                        op0=ALU.mult,
-                        op1=ALU.add,
-                    )
-                for cb in range(N_CB):
-                    nc.scalar.activation(
-                        out=image[:, cb, cols],
-                        in_=summed[:, cb, :],
-                        func=ACT.Relu,
-                        bias=b_col[:, cb : cb + 1],
-                        scale=1.0,
-                    )
-                    if i == N_TILES - 1:
-                        nc.sync.dma_start(out=out_view[:, b, cb, :], in_=image[:, cb, :])
-                return
-            result = work.tile([P, N_CB, P], F32)
+        def pixel_cols(i):
+            return slice((i % 2) * P, (i % 2 + 1) * P)
+
+        def scale_and_add(i, blocks):
             for cb in range(N_CB):
                 nc.vector.scalar_tensor_tensor(
-                    out=summed[:, cb, :],
+                    out=summed[i][:, cb, :],
                     in0=blocks[cb][:],
                     scalar=w_col[:, cb : cb + 1],
-                    in1=x_sb[:, b * N_CB + cb, cols],
+                    in1=x_sb[:, (i // 2) * N_CB + cb, pixel_cols(i)],
                     op0=ALU.mult,
                     op1=ALU.add,
                 )
-            for cb in range(HALF):
-                nc.scalar.activation(
-                    out=result[:, cb, :], in_=summed[:, cb, :], func=ACT.Relu, bias=b_col[:, cb : cb + 1], scale=1.0
+
+        def add_and_relu(i, cb):
+            if i == N_TILES - 1 and cb % 2 == 1:
+                nc.vector.tensor_scalar(
+                    out=result[:, i // 2, cb, pixel_cols(i)],
+                    in0=summed[i][:, cb, :],
+                    scalar1=b_col[:, cb : cb + 1],
+                    scalar2=0.0,
+                    op0=ALU.add,
+                    op1=ALU.max,
                 )
-            nc.sync.dma_start(out=out_view[:, b, 0:HALF, cols], in_=result[:, 0:HALF, :])
-            for cb in range(HALF, N_CB):
-                nc.scalar.activation(
-                    out=result[:, cb, :], in_=summed[:, cb, :], func=ACT.Relu, bias=b_col[:, cb : cb + 1], scale=1.0
-                )
-            nc.sync.dma_start(out=out_view[:, b, HALF:N_CB, cols], in_=result[:, HALF:N_CB, :])
+                return
+            nc.scalar.activation(
+                out=result[:, i // 2, cb, pixel_cols(i)],
+                in_=summed[i][:, cb, :],
+                func=ACT.Relu,
+                bias=b_col[:, cb : cb + 1],
+                scale=1.0,
+            )
+
+        def store(i, cbs, cols):
+            nc.sync.dma_start(out=out_view[:, i // 2, cbs, cols], in_=result[:, i // 2, cbs, cols])
+
+        def finish(i):
+            for cb in range(N_CB):
+                add_and_relu(i, cb)
+                if i < 2 and cb % HALF == HALF - 1:
+                    store(i, slice(cb + 1 - HALF, cb + 1), pixel_cols(i))
+                if i == N_TILES - 1:
+                    store(i, slice(cb, cb + 1), slice(0, IMAGE))
 
         g0 = turn(0)
-        bias_ps = spread_bias()
         quantise(0, g0)
-        nc.vector.tensor_copy(out=bias_sb[:], in_=bias_ps[:])
         g1 = turn(1)
-        g2 = turn(2)
-        g3 = turn(3)
+        bias_ps = spread_bias()
+        nc.vector.tensor_copy(out=bias_sb[:], in_=bias_ps[:])
         quantise(1, g1)
-        quantise(2, g2)
         acc0 = multiply(0)
         add_bias(0, acc0)
-        quantise(3, g3)
+        g2 = turn(2)
+        quantise(2, g2)
+        g3 = turn(3)
         acc1 = multiply(1)
         add_bias(1, acc1)
+        quantise(3, g3)
         acc2 = multiply(2)
         add_bias(2, acc2)
+        channel_columns()
         acc3 = multiply(3)
         add_bias(3, acc3)
-        channel_columns()
-        for i in range(N_TILES):
-            sum_squares(i)
-        for i in range(N_TILES):
-            finish(i, normalise_and_turn(i))
+        for i in range(2):
+            inverse_deviation(i, sum_squares(i))
+            normalise(i, nc.gpsimd)
+        ssd2 = sum_squares(2)
+        ssd3 = sum_squares(3)
+        inverse_deviation(2, ssd2)
+        inverse_deviation(3, ssd3)
+        normalise(3, nc.gpsimd)
+        scale_and_add(0, turn_back(0))
+        normalise(2, nc.vector)
+        finish(0)
+        scale_and_add(1, turn_back(1))
+        finish(1)
+        scale_and_add(2, turn_back(2))
+        finish(2)
+        scale_and_add(3, turn_back(3))
+        finish(3)

@@ -31,8 +31,8 @@ def tile_transformerconvblock_pc_s_kernel(
 ):
     nc = tc.nc
     h_rows = h.rearrange("b i j f -> (b i j) f")
-    x_view = x.rearrange("b (cb p) i j -> p (b cb) (i j)", p=P)
-    out_view = out.rearrange("b (cb p) i j -> p b cb (i j)", p=P)
+    x_view = x.rearrange("b (p cb) i j -> p b (cb i j)", cb=N_CB)
+    out_view = out.rearrange("b (p cb) i j -> p b cb (i j)", cb=N_CB)
 
     with ExitStack() as ctx:
         keep = ctx.enter_context(tc.tile_pool(name="keep", bufs=1))
@@ -43,24 +43,21 @@ def tile_transformerconvblock_pc_s_kernel(
         h_sb = keep.tile([P, N_TILES, K], BF16)
         w_words = keep.tile([P, 2 * C], U8, align_bytes=64)
         w_plane = keep.tile([P, C], U8, align_bytes=64)
-        x_sb = keep.tile([P, 2 * N_CB, IMAGE], BF16)
-        bias_row = keep.tile([P, C], BF16)
-        ln_rows = keep.tile([P, P], BF16)
+        x_sb = keep.tile([P, 2, N_CB * IMAGE], BF16)
+        ffn2_b_sb = keep.tile([P, N_CB], BF16)
+        ln2_w_sb = keep.tile([P, N_CB], BF16)
+        ln2_b_sb = keep.tile([P, N_CB], BF16)
         s_ffn = keep.tile([P, 1], BF16)
         s_norm = keep.tile([P, 1], BF16)
-        ones = keep.tile([P, P], BF16)
         one_col = keep.tile([P, 1], F32)
         warm_sb = keep.tile([P, P], F32)
 
         nc.vector.memset(warm_sb[:], 1.0)
-        nc.vector.memset(bias_row[:].bitcast(F32), 0.0)
         nc.vector.memset(w_plane[:].bitcast(I32), 0)
         nc.vector.memset(one_col[:], 1.0)
-        nc.vector.memset(ones[:], 1.0)
-        nc.vector.memset(ln_rows[:], 0.0)
 
         nc.sync.dma_start(out=h_sb[:, 0, :], in_=h_rows[0:P, :])
-        nc.scalar.dma_start(out=bias_row[0:1, :], in_=ffn2_b.unsqueeze(0))
+        nc.scalar.dma_start(out=ffn2_b_sb[:], in_=ffn2_b.rearrange("(p cb) -> p cb", cb=N_CB))
         nc.sync.dma_start(
             out=h_sb[:, 1:N_TILES, :], in_=h_rows[P:PIXELS, :].rearrange("(t p) k -> p t k", p=P)
         )
@@ -70,8 +67,8 @@ def tile_transformerconvblock_pc_s_kernel(
             nc.sync.dma_start(out=w_plane[r:P:32, :].bitcast(I32), in_=scale_rows[r:16:4, :])
         nc.sync.dma_start(out=s_ffn[:], in_=scale_ffn.partition_broadcast(P))
         nc.sync.dma_start(out=s_norm[:], in_=scale_norm2.partition_broadcast(P))
-        nc.sync.dma_start(out=ln_rows[0:N_CB, :], in_=ln2_w.rearrange("(cb c) -> cb c", c=P))
-        nc.sync.dma_start(out=ln_rows[N_CB : 2 * N_CB, :], in_=ln2_b.rearrange("(cb c) -> cb c", c=P))
+        nc.sync.dma_start(out=ln2_w_sb[:], in_=ln2_w.rearrange("(p cb) -> p cb", cb=N_CB))
+        nc.sync.dma_start(out=ln2_b_sb[:], in_=ln2_b.rearrange("(p cb) -> p cb", cb=N_CB))
         nc.sync.dma_start(out=x_sb[:], in_=x_view)
 
         ident_f32 = keep.tile([P, P], F32)
@@ -79,11 +76,14 @@ def tile_transformerconvblock_pc_s_kernel(
         make_identity(nc, ident_f32[:])
         make_identity(nc, ident_bf[:])
 
-        for width in (P, P, 44):
+        def keep_busy(width):
             warm_ps = psum.tile([P, P], F32, tag="bank")
             nc.tensor.matmul(
                 out=warm_ps[:, 0:width], lhsT=warm_sb[:], rhs=warm_sb[:, 0:width], start=True, stop=True
             )
+
+        for width in (P, P, 44):
+            keep_busy(width)
 
         warm = keep.tile([P, 1], F32)
         nc.scalar.activation(out=warm[:], in_=one_col[:], func=ACT.Abs_reciprocal_sqrt)
@@ -98,13 +98,20 @@ def tile_transformerconvblock_pc_s_kernel(
         )
 
         result = keep.tile([P, 2, N_CB, IMAGE], F32)
+        w_col = keep.tile([P, N_CB], F32)
+        nc.gpsimd.tensor_scalar(
+            out=w_col[:], in0=ln2_w_sb[:], scalar1=gain[:, 0:1], scalar2=0.0, op0=ALU.mult, op1=ALU.add
+        )
+        b_col = keep.tile([P, N_CB], F32)
+        nc.gpsimd.tensor_scalar(
+            out=b_col[:], in0=ln2_b_sb[:], scalar1=s_norm[:, 0:1], scalar2=0.0, op0=ALU.mult, op1=ALU.add
+        )
+
         h_codes = keep.tile([P, N_TILES, P], U32, align_bytes=64)
         h_scales = keep.tile([P, N_TILES, P], U8, align_bytes=64)
-        bias_sb = keep.tile([P, C], BF16)
-        w_col = keep.tile([P, N_CB], F32)
-        b_col = keep.tile([P, N_CB], F32)
-        v = [work.tile([P, C], F32, name="v") for i in range(N_TILES)]
-        zn = [work.tile([P, C], F32, name="zn") for i in range(N_TILES)]
+        bias_sb = keep.tile([P, N_CB, P], BF16)
+        v = [work.tile([P, N_CB, P], F32, name="v") for i in range(N_TILES)]
+        zn = [work.tile([P, N_CB, P], F32, name="zn") for i in range(N_TILES)]
         summed = [work.tile([P, N_CB, P], F32, name="summed") for i in range(N_TILES)]
         v_sum = [work.tile([P, 1], F32, name="v_sum") for i in range(N_TILES)]
         neg_mean = [work.tile([P, 1], F32, name="neg_mean") for i in range(N_TILES)]
@@ -128,8 +135,11 @@ def tile_transformerconvblock_pc_s_kernel(
             )
 
         def spread_bias():
-            bias_ps = psum.tile([P, C], BF16, tag="bank")
-            nc.tensor.matmul(out=bias_ps[:], lhsT=ones[:], rhs=bias_row[:], start=True, stop=True)
+            bias_ps = psum.tile([P, N_CB, P], BF16, tag="bank")
+            for cb in range(N_CB):
+                nc.tensor.transpose(
+                    bias_ps[:, cb, :], ffn2_b_sb[:, cb : cb + 1].to_broadcast([P, P]), ident_bf[:]
+                )
             return bias_ps
 
         def multiply(i):
@@ -147,21 +157,17 @@ def tile_transformerconvblock_pc_s_kernel(
 
         def add_bias(i, acc):
             nc.vector.scalar_tensor_tensor(
-                out=v[i][:], in0=acc[:], scalar=1.0, in1=bias_sb[:], op0=ALU.mult, op1=ALU.add, accum_out=v_sum[i][:]
-            )
-
-        def channel_columns():
-            ln_ps = psum.tile([P, P], BF16, tag="bank")
-            nc.tensor.transpose(ln_ps[:], ln_rows[:], ident_bf[:])
-            nc.vector.tensor_scalar(
-                out=w_col[:], in0=ln_ps[:, 0:N_CB], scalar1=gain[:, 0:1], scalar2=None, op0=ALU.mult
-            )
-            nc.vector.tensor_scalar(
-                out=b_col[:], in0=ln_ps[:, N_CB : 2 * N_CB], scalar1=s_norm[:, 0:1], scalar2=None, op0=ALU.mult
+                out=v[i][:],
+                in0=acc[:].rearrange("p (j cb) -> p cb j", cb=N_CB),
+                scalar=1.0,
+                in1=bias_sb[:],
+                op0=ALU.mult,
+                op1=ALU.add,
+                accum_out=v_sum[i][:],
             )
 
         def sum_squares(i):
-            squares = work.tile([P, C], F32)
+            squares = work.tile([P, N_CB, P], F32)
             ssd = work.tile([P, 1], F32)
             nc.scalar.activation(
                 out=squares[:], in_=v[i][:], func=ACT.Square, bias=v_sum[i][:], scale=-1.0 * C, accum_out=ssd[:]
@@ -174,10 +180,10 @@ def tile_transformerconvblock_pc_s_kernel(
                 out=r_hat[i][:], in_=ssd[:], func=ACT.Abs_reciprocal_sqrt, bias=one_col[:], scale=k_col[:]
             )
 
-        def normalise(i, engine, cols=slice(0, C)):
+        def normalise(i, engine):
             engine.tensor_scalar(
-                out=zn[i][:, cols],
-                in0=v[i][:, cols],
+                out=zn[i][:],
+                in0=v[i][:],
                 scalar1=neg_mean[i][:, 0:1],
                 scalar2=r_hat[i][:, 0:1],
                 op0=ALU.add,
@@ -188,7 +194,7 @@ def tile_transformerconvblock_pc_s_kernel(
             blocks = []
             for cb in range(N_CB):
                 znT_ps = psum.tile([P, P], F32, tag="bank")
-                nc.tensor.transpose(znT_ps[:], zn[i][:, cb * P : (cb + 1) * P], ident_f32[:])
+                nc.tensor.transpose(znT_ps[:], zn[i][:, cb, :], ident_f32[:])
                 blocks.append(znT_ps)
             return blocks
 
@@ -201,7 +207,7 @@ def tile_transformerconvblock_pc_s_kernel(
                     out=summed[i][:, cb, :],
                     in0=blocks[cb][:],
                     scalar=w_col[:, cb : cb + 1],
-                    in1=x_sb[:, (i // 2) * N_CB + cb, pixel_cols(i)],
+                    in1=x_sb[:, i // 2, cb * IMAGE + (i % 2) * P : cb * IMAGE + (i % 2 + 1) * P],
                     op0=ALU.mult,
                     op1=ALU.add,
                 )
@@ -238,9 +244,10 @@ def tile_transformerconvblock_pc_s_kernel(
 
         g0 = turn(0)
         quantise(0, g0)
-        g1 = turn(1)
         bias_ps = spread_bias()
         nc.vector.tensor_copy(out=bias_sb[:], in_=bias_ps[:])
+        keep_busy(P)
+        g1 = turn(1)
         quantise(1, g1)
         acc0 = multiply(0)
         add_bias(0, acc0)
@@ -252,9 +259,9 @@ def tile_transformerconvblock_pc_s_kernel(
         quantise(3, g3)
         acc2 = multiply(2)
         add_bias(2, acc2)
-        channel_columns()
         acc3 = multiply(3)
         add_bias(3, acc3)
+        keep_busy(P)
         for i in range(2):
             inverse_deviation(i, sum_squares(i))
             normalise(i, nc.gpsimd)
@@ -266,8 +273,10 @@ def tile_transformerconvblock_pc_s_kernel(
         scale_and_add(0, turn_back(0))
         normalise(2, nc.vector)
         finish(0)
+        keep_busy(P)
         scale_and_add(1, turn_back(1))
         finish(1)
+        keep_busy(P)
         scale_and_add(2, turn_back(2))
         finish(2)
         scale_and_add(3, turn_back(3))

@@ -56,11 +56,10 @@ def tile_transformerconvblock_pc_s_kernel(
         nc.vector.memset(w_plane[:].bitcast(I32), 0)
         nc.vector.memset(one_col[:], 1.0)
 
-        nc.sync.dma_start(out=h_sb[:, 0, :], in_=h_rows[0:P, :])
+        h_tiles = h_rows.rearrange("(t p) k -> p t k", p=P)
+        nc.sync.dma_start(out=h_sb[:, 0:2, :], in_=h_tiles[:, 0:2, :])
         nc.scalar.dma_start(out=ffn2_b_sb[:], in_=ffn2_b.rearrange("(p cb) -> p cb", cb=N_CB))
-        nc.sync.dma_start(
-            out=h_sb[:, 1:N_TILES, :], in_=h_rows[P:PIXELS, :].rearrange("(t p) k -> p t k", p=P)
-        )
+        nc.sync.dma_start(out=h_sb[:, 2:N_TILES, :], in_=h_tiles[:, 2:N_TILES, :])
         nc.sync.dma_start(out=w_words[:].bitcast(I32), in_=ffn2_w_words[0].bitcast(I32))
         scale_rows = ffn2_w_scales[0].bitcast(I32)
         for r in range(4):
@@ -82,7 +81,7 @@ def tile_transformerconvblock_pc_s_kernel(
                 out=warm_ps[:, 0:width], lhsT=warm_sb[:], rhs=warm_sb[:, 0:width], start=True, stop=True
             )
 
-        for width in (P, P, 44):
+        for width in (P, P, 104):
             keep_busy(width)
 
         warm = keep.tile([P, 1], F32)
@@ -244,14 +243,14 @@ def tile_transformerconvblock_pc_s_kernel(
 
         g0 = turn(0)
         quantise(0, g0)
-        bias_ps = spread_bias()
-        nc.vector.tensor_copy(out=bias_sb[:], in_=bias_ps[:])
         keep_busy(P)
         g1 = turn(1)
         quantise(1, g1)
+        bias_ps = spread_bias()
+        nc.vector.tensor_copy(out=bias_sb[:], in_=bias_ps[:])
+        g2 = turn(2)
         acc0 = multiply(0)
         add_bias(0, acc0)
-        g2 = turn(2)
         quantise(2, g2)
         g3 = turn(3)
         acc1 = multiply(1)
@@ -276,7 +275,7 @@ def tile_transformerconvblock_pc_s_kernel(
         keep_busy(P)
         scale_and_add(1, turn_back(1))
         finish(1)
-        keep_busy(P)
+        keep_busy(72)
         scale_and_add(2, turn_back(2))
         finish(2)
         scale_and_add(3, turn_back(3))

from contextlib import ExitStack

import concourse.mybir as mybir
from concourse.masks import make_identity

F32 = mybir.dt.float32
BF16 = mybir.dt.bfloat16
I32 = mybir.dt.int32
U32 = mybir.dt.uint32
U8 = mybir.dt.uint8
FP8X4 = mybir.dt.float8_e4m3fn_x4
FP4X4 = mybir.dt.float4_e2m1fn_x4
ALU = mybir.AluOpType
ACT = mybir.ActivationFunctionType

P = 128
K = 512
C = 512
PIXELS = 512
IMAGE = 256
N_TILES = PIXELS // P
N_CB = C // P
HALF = N_CB // 2
EPS = 1e-5

FLOPS = 2 * PIXELS * K * C


def tile_transformerconvblock_pc_s_kernel(
    tc, h, ffn2_w_words, ffn2_w_scales, ffn2_b, scale_ffn, ln2_w, ln2_b, scale_norm2, x, out
):
    nc = tc.nc
    h_rows = h.rearrange("b i j f -> (b i j) f")
    x_view = x.rearrange("b (p cb) i j -> p b (cb i j)", cb=N_CB)
    out_view = out.rearrange("b (p cb) i j -> p b cb (i j)", cb=N_CB)

    with ExitStack() as ctx:
        keep = ctx.enter_context(tc.tile_pool(name="keep", bufs=1))
        work = ctx.enter_context(tc.tile_pool(name="work", bufs=N_TILES))
        psum = ctx.enter_context(tc.psum_pool(name="psum", bufs=8))
        ctx.enter_context(tc.manual_schedule())

        h_sb = keep.tile([P, N_TILES, K], BF16)
        w_words = keep.tile([P, 2 * C], U8, align_bytes=64)
        w_plane = keep.tile([P, C], U8, align_bytes=64)
        x_sb = keep.tile([P, 2, N_CB * IMAGE], BF16)
        ffn2_b_sb = keep.tile([P, N_CB], BF16)
        ln2_w_sb = keep.tile([P, N_CB], BF16)
        ln2_b_sb = keep.tile([P, N_CB], BF16)
        s_ffn = keep.tile([P, 1], BF16)
        s_norm = keep.tile([P, 1], BF16)
        one_col = keep.tile([P, 1], F32)
        warm_sb = keep.tile([P, P], F32)

        nc.vector.memset(warm_sb[:], 1.0)
        nc.vector.memset(w_plane[:].bitcast(I32), 0)
        nc.vector.memset(one_col[:], 1.0)

        h_tiles = h_rows.rearrange("(t p) k -> p t k", p=P)
        nc.sync.dma_start(out=h_sb[:, 0:2, :], in_=h_tiles[:, 0:2, :])
        nc.scalar.dma_start(out=ffn2_b_sb[:], in_=ffn2_b.rearrange("(p cb) -> p cb", cb=N_CB))
        nc.sync.dma_start(out=h_sb[:, 2:N_TILES, :], in_=h_tiles[:, 2:N_TILES, :])
        nc.sync.dma_start(out=w_words[:].bitcast(I32), in_=ffn2_w_words[0].bitcast(I32))
        scale_rows = ffn2_w_scales[0].bitcast(I32)
        for r in range(4):
            nc.sync.dma_start(out=w_plane[r:P:32, :].bitcast(I32), in_=scale_rows[r:16:4, :])
        nc.sync.dma_start(out=s_ffn[:], in_=scale_ffn.partition_broadcast(P))
        nc.sync.dma_start(out=s_norm[:], in_=scale_norm2.partition_broadcast(P))
        nc.sync.dma_start(out=ln2_w_sb[:], in_=ln2_w.rearrange("(p cb) -> p cb", cb=N_CB))
        nc.sync.dma_start(out=ln2_b_sb[:], in_=ln2_b.rearrange("(p cb) -> p cb", cb=N_CB))
        nc.sync.dma_start(out=x_sb[:], in_=x_view)

        ident_f32 = keep.tile([P, P], F32)
        ident_bf = keep.tile([P, P], BF16)
        make_identity(nc, ident_f32[:])
        make_identity(nc, ident_bf[:])

        def keep_busy(width):
            warm_ps = psum.tile([P, P], F32, tag="bank")
            nc.tensor.matmul(
                out=warm_ps[:, 0:width], lhsT=warm_sb[:], rhs=warm_sb[:, 0:width], start=True, stop=True
            )

        for width in (P, P, 104):
            keep_busy(width)

        warm = keep.tile([P, 1], F32)
        nc.scalar.activation(out=warm[:], in_=one_col[:], func=ACT.Abs_reciprocal_sqrt)

        k_col = keep.tile([P, 1], F32)
        nc.gpsimd.tensor_scalar(
            out=k_col[:], in0=s_ffn[:], scalar1=s_ffn[:, 0:1], scalar2=1.0 / (C**3 * EPS), op0=ALU.mult, op1=ALU.mult
        )
        gain = keep.tile([P, 1], F32)
        nc.gpsimd.tensor_scalar(
            out=gain[:], in0=s_ffn[:], scalar1=s_norm[:, 0:1], scalar2=EPS**-0.5, op0=ALU.mult, op1=ALU.mult
        )

        result = keep.tile([P, 2, N_CB, IMAGE], F32)
        w_col = keep.tile([P, N_CB], F32)
        nc.gpsimd.tensor_scalar(
            out=w_col[:], in0=ln2_w_sb[:], scalar1=gain[:, 0:1], scalar2=0.0, op0=ALU.mult, op1=ALU.add
        )
        b_col = keep.tile([P, N_CB], F32)
        nc.gpsimd.tensor_scalar(
            out=b_col[:], in0=ln2_b_sb[:], scalar1=s_norm[:, 0:1], scalar2=0.0, op0=ALU.mult, op1=ALU.add
        )

        h_codes = keep.tile([P, N_TILES, P], U32, align_bytes=64)
        h_scales = keep.tile([P, N_TILES, P], U8, align_bytes=64)
        bias_sb = keep.tile([P, N_CB, P], BF16)
        v = [work.tile([P, N_CB, P], F32, name="v") for i in range(N_TILES)]
        zn = [work.tile([P, N_CB, P], F32, name="zn") for i in range(N_TILES)]
        summed = [work.tile([P, N_CB, P], F32, name="summed") for i in range(N_TILES)]
        v_sum = [work.tile([P, 1], F32, name="v_sum") for i in range(N_TILES)]
        neg_mean = [work.tile([P, 1], F32, name="neg_mean") for i in range(N_TILES)]
        r_hat = [work.tile([P, 1], F32, name="r_hat") for i in range(N_TILES)]

        def turn(i):
            h_words = h_sb[:, i, :].bitcast(F32)
            hT_ps = psum.tile([P, 2, P], F32, tag="bank")
            for u in range(2):
                nc.tensor.transpose(hT_ps[:, u, :], h_words[:, u : K // 2 : 2], ident_f32[:])
            grouped = work.tile([P, 4 * P], BF16, align_bytes=64)
            nc.scalar.copy(
                out=grouped[:].bitcast(F32).rearrange("p (r u) -> p r u", u=2),
                in_=hT_ps[:].rearrange("p u r -> p r u"),
            )
            return grouped

        def quantise(i, grouped):
            nc.vector.quantize_mx(
                out=h_codes[:, i, :].bitcast(FP8X4), scales=h_scales[:, i, :], in_=grouped[:]
            )

        def spread_bias():
            bias_ps = psum.tile([P, N_CB, P], BF16, tag="bank")
            for cb in range(N_CB):
                nc.tensor.transpose(
                    bias_ps[:, cb, :], ffn2_b_sb[:, cb : cb + 1].to_broadcast([P, P]), ident_bf[:]
                )
            return bias_ps

        def multiply(i):
            acc = psum.tile([P, C], F32, tag="bank")
            nc.tensor.matmul_mx(
                out=acc[:],
                lhsT=h_codes[:, i, :].bitcast(FP8X4),
                lhsT_scale=h_scales[:, i, :],
                rhs=w_words[:].bitcast(FP4X4),
                rhs_scale=w_plane[:],
                start=True,
                stop=True,
            )
            return acc

        def add_bias(i, acc):
            nc.vector.scalar_tensor_tensor(
                out=v[i][:],
                in0=acc[:].rearrange("p (j cb) -> p cb j", cb=N_CB),
                scalar=1.0,
                in1=bias_sb[:],
                op0=ALU.mult,
                op1=ALU.add,
                accum_out=v_sum[i][:],
            )

        def sum_squares(i):
            squares = work.tile([P, N_CB, P], F32)
            ssd = work.tile([P, 1], F32)
            nc.scalar.activation(
                out=squares[:], in_=v[i][:], func=ACT.Square, bias=v_sum[i][:], scale=-1.0 * C, accum_out=ssd[:]
            )
            nc.scalar.mul(out=neg_mean[i][:], in_=v_sum[i][:], mul=-1.0 / C)
            return ssd

        def inverse_deviation(i, ssd):
            nc.scalar.activation(
                out=r_hat[i][:], in_=ssd[:], func=ACT.Abs_reciprocal_sqrt, bias=one_col[:], scale=k_col[:]
            )

        def normalise(i, engine):
            engine.tensor_scalar(
                out=zn[i][:],
                in0=v[i][:],
                scalar1=neg_mean[i][:, 0:1],
                scalar2=r_hat[i][:, 0:1],
                op0=ALU.add,
                op1=ALU.mult,
            )

        def turn_back(i):
            blocks = []
            for cb in range(N_CB):
                znT_ps = psum.tile([P, P], F32, tag="bank")
                nc.tensor.transpose(znT_ps[:], zn[i][:, cb, :], ident_f32[:])
                blocks.append(znT_ps)
            return blocks

        def pixel_cols(i):
            return slice((i % 2) * P, (i % 2 + 1) * P)

        def scale_and_add(i, blocks):
            for cb in range(N_CB):
                nc.vector.scalar_tensor_tensor(
                    out=summed[i][:, cb, :],
                    in0=blocks[cb][:],
                    scalar=w_col[:, cb : cb + 1],
                    in1=x_sb[:, i // 2, cb * IMAGE + (i % 2) * P : cb * IMAGE + (i % 2 + 1) * P],
                    op0=ALU.mult,
                    op1=ALU.add,
                )

        def add_and_relu(i, cb):
            if i == N_TILES - 1 and cb % 2 == 1:
                nc.vector.tensor_scalar(
                    out=result[:, i // 2, cb, pixel_cols(i)],
                    in0=summed[i][:, cb, :],
                    scalar1=b_col[:, cb : cb + 1],
                    scalar2=0.0,
                    op0=ALU.add,
                    op1=ALU.max,
                )
                return
            nc.scalar.activation(
                out=result[:, i // 2, cb, pixel_cols(i)],
                in_=summed[i][:, cb, :],
                func=ACT.Relu,
                bias=b_col[:, cb : cb + 1],
                scale=1.0,
            )

        def store(i, cbs, cols):
            nc.sync.dma_start(out=out_view[:, i // 2, cbs, cols], in_=result[:, i // 2, cbs, cols])

        def finish(i):
            for cb in range(N_CB):
                add_and_relu(i, cb)
                if i < 2 and cb % HALF == HALF - 1:
                    store(i, slice(cb + 1 - HALF, cb + 1), pixel_cols(i))
                if i == N_TILES - 1:
                    store(i, slice(cb, cb + 1), slice(0, IMAGE))

        g0 = turn(0)
        quantise(0, g0)
        keep_busy(P)
        g1 = turn(1)
        quantise(1, g1)
        bias_ps = spread_bias()
        nc.vector.tensor_copy(out=bias_sb[:], in_=bias_ps[:])
        g2 = turn(2)
        acc0 = multiply(0)
        add_bias(0, acc0)
        quantise(2, g2)
        g3 = turn(3)
        acc1 = multiply(1)
        add_bias(1, acc1)
        quantise(3, g3)
        acc2 = multiply(2)
        add_bias(2, acc2)
        acc3 = multiply(3)
        add_bias(3, acc3)
        keep_busy(P)
        for i in range(2):
            inverse_deviation(i, sum_squares(i))
            normalise(i, nc.gpsimd)
        ssd2 = sum_squares(2)
        ssd3 = sum_squares(3)
        inverse_deviation(2, ssd2)
        inverse_deviation(3, ssd3)
        normalise(3, nc.gpsimd)
        scale_and_add(0, turn_back(0))
        normalise(2, nc.vector)
        finish(0)
        keep_busy(P)
        scale_and_add(1, turn_back(1))
        finish(1)
        keep_busy(72)
        scale_and_add(2, turn_back(2))
        finish(2)
        scale_and_add(3, turn_back(3))
        finish(3)
